import numpy as np
import ml_dtypes


def mxq(x, axis, fmt="e4m3"):
    dtype, down = {"e4m3": (ml_dtypes.float8_e4m3fn, 7), "e5m2": (ml_dtypes.float8_e5m2, 14)}[fmt]
    v = np.moveaxis(np.asarray(x, np.float32).astype(ml_dtypes.bfloat16).astype(np.float64), axis, -1)
    blocks = v.reshape(v.shape[:-1] + (-1, 32))
    amax = np.abs(blocks).max(-1, keepdims=True)
    byte = np.maximum(np.where(amax > 0, np.frexp(amax)[1] - 1 + 127, 0) - down, 1)
    scale = np.exp2(byte - 127.0)
    codes = (blocks / scale).astype(np.float32).astype(dtype).astype(np.float64)
    return np.moveaxis((codes * scale).reshape(v.shape), -1, axis)


WIDE = False


def mx_kscale(k):
    if not WIDE:
        return np.ones(k)
    levels = np.array([10, -10, 5, -5, 0])
    if k % 512:
        return np.exp2(np.random.permutation(np.resize(levels, k // 32))).repeat(32)
    a = np.empty((k // 512, 16))
    for p in range(k // 512):
        a[p, :8] = np.random.permutation(np.resize(levels, 8))
        for g in range(8):
            far = levels[np.abs(levels - a[p, g]) >= 10]
            a[p, g + 8] = far[np.random.randint(len(far))]
    return np.exp2(a.ravel()).repeat(32)


BF16 = ml_dtypes.bfloat16


def bf(x):
    return np.asarray(x, np.float32).astype(BF16)


def f64(x):
    return np.asarray(x).astype(np.float64)


B, S, D, DR = 2, 512, 1024, 1024
G = 1.4 * (D / DR) ** 0.25 / np.sqrt(D)


def setup_inputs():
    s = mx_kscale(D)
    t = mx_kscale(DR)
    mask = (np.random.random((S, S)) < 0.5) & ~np.eye(S, dtype=bool)
    return {"q_lin": bf(np.random.standard_normal((B, S, D)) * s),
            "k_lin": bf(np.random.standard_normal((B, S, D)) * s),
            "rotation_params": bf(np.random.standard_normal((DR, D)) * G * t[:, None] / s),
            "entangle_params": bf(np.random.standard_normal((DR, D)) * G / t[:, None] / s),
            "mask": mask}


def reference(q_lin, k_lin, rotation_params, entangle_params, mask):
    q = mxq(f64(q_lin), 2, "e4m3") @ mxq(f64(rotation_params), 1, "e4m3").T
    k = mxq(f64(k_lin), 2, "e4m3") @ mxq(f64(entangle_params), 1, "e4m3").T
    scores = (mxq(q, 2, "e4m3") @ mxq(k, 2, "e4m3").transpose(0, 2, 1)) / np.sqrt(D)
    scores = np.where(f64(mask) > 0.5, -np.inf, scores)
    e = np.exp(scores - scores.max(-1, keepdims=True))
    return e / e.sum(-1, keepdims=True)

@@ -1,0 +1,246 @@
+from contextlib import ExitStack
+
+import concourse.mybir as mybir
+from concourse.masks import make_identity
+
+F32 = mybir.dt.float32
+BF16 = mybir.dt.bfloat16
+I32 = mybir.dt.int32
+U32 = mybir.dt.uint32
+U8 = mybir.dt.uint8
+FP8X4 = mybir.dt.float8_e4m3fn_x4
+ALU = mybir.AluOpType
+ACT = mybir.ActivationFunctionType
+AXIS = mybir.AxisListType
+
+B, S, D, DR = 2, 512, 1024, 1024
+P = 128
+PACK = 4
+K_PASS = P * PACK
+BANK = 512
+D_PASSES = D // K_PASS
+DR_PASSES = DR // K_PASS
+TILES = 4
+ROW_WORDS = D // 2
+QUERY_TILES = B * TILES
+AHEAD = 2
+FAR = 1.5e38
+SCORE_SCALE = D**-0.5
+assert SCORE_SCALE == 2.0**-5
+
+FLOPS = 2 * (2 * B * S * D * DR) + 2 * B * S * S * DR
+
+
+def tile_selfattention_pa_kernel(tc, q_lin, k_lin, rotation_params, entangle_params, mask, out):
+    nc = tc.nc
+    with ExitStack() as ctx:
+        keep = ctx.enter_context(tc.tile_pool(name="keep", bufs=1))
+        stage = ctx.enter_context(tc.tile_pool(name="stage", bufs=3))
+        soft = ctx.enter_context(tc.tile_pool(name="soft", bufs=3))
+        small = ctx.enter_context(tc.tile_pool(name="small", bufs=4))
+        psum = ctx.enter_context(tc.psum_pool(name="psum", bufs=8))
+        ctx.enter_context(tc.manual_schedule())
+
+        def load_chunk(name, rows_of_partition):
+            chunk = keep.tile([P, TILES * D], BF16, name=name)
+            for i in range(TILES):
+                nc.sync.dma_start(out=chunk[:, i * D : (i + 1) * D], in_=rows_of_partition[:, i, :])
+            return chunk
+
+        def weight_rows(w, h):
+            return w.rearrange("(h p i) d -> h p i d", h=DR_PASSES, i=TILES)[h]
+
+        def token_rows(x, b):
+            return x[b].rearrange("(i p) d -> p i d", p=P)
+
+        ent_rows = [None] * DR_PASSES
+        rot_rows = [None] * DR_PASSES
+        k_rows = [None] * B
+        q_rows = [None] * B
+        ent_rows[0] = load_chunk("ent_rows0", weight_rows(entangle_params, 0))
+        k_rows[0] = load_chunk("k_rows0", token_rows(k_lin, 0))
+        ent_rows[1] = load_chunk("ent_rows1", weight_rows(entangle_params, 1))
+        rot_rows[0] = load_chunk("rot_rows0", weight_rows(rotation_params, 0))
+        rot_rows[1] = load_chunk("rot_rows1", weight_rows(rotation_params, 1))
+        q_rows[0] = load_chunk("q_rows0", token_rows(q_lin, 0))
+        k_rows[1] = load_chunk("k_rows1", token_rows(k_lin, 1))
+        q_rows[1] = load_chunk("q_rows1", token_rows(q_lin, 1))
+        mask_words = keep.tile([P, TILES, 2 * S], I32, name="mask_words")
+        for j in range(TILES):
+            nc.sync.dma_start(out=mask_words[:, j, :], in_=mask.bitcast(I32)[j * P : (j + 1) * P, :])
+
+        ident = keep.tile([P, P], F32, name="ident")
+        make_identity(nc, ident[:])
+
+        zero = small.tile([P, 1], F32, name="zero")
+        one = small.tile([P, 1], F32, name="one")
+        nc.vector.memset(zero[:], 0.0)
+        nc.scalar.activation(out=one[:], in_=zero[:], func=ACT.Exp)
+
+        def new_operand(name, shape):
+            codes = keep.tile([P] + shape, U32, name=name + "_codes", align_bytes=64)
+            scales = keep.tile([P] + shape, U8, name=name + "_scales", align_bytes=64)
+            return codes, scales
+
+        ent = [new_operand("ent%d" % h, [TILES, D_PASSES, P]) for h in range(DR_PASSES)]
+        rot = [new_operand("rot%d" % h, [TILES, D_PASSES, P]) for h in range(DR_PASSES)]
+        k_tok = [new_operand("k_tok%d" % b, [TILES, D_PASSES, P]) for b in range(B)]
+        q_tok = [new_operand("q_tok%d" % b, [TILES, D_PASSES, P]) for b in range(B)]
+        k_mx = new_operand("k", [B, DR_PASSES, S])
+        q_mx = new_operand("q", [B, DR_PASSES, S])
+
+        def quantise_chunk(chunk, operand):
+            codes, scales = operand
+            words = chunk[:].bitcast(F32)
+            grouped = stage.tile([P, TILES * D], BF16, tag="grouped_rows", align_bytes=64)
+            grouped_words = grouped[:].bitcast(F32)
+            for i in range(TILES):
+                bank = psum.tile([P, BANK], F32, tag="bank")
+                for c in range(ROW_WORDS // P):
+                    g, u = c // 2, c % 2
+                    start = i * ROW_WORDS + g * 2 * P
+                    nc.tensor.transpose(
+                        bank[:, c * P : (c + 1) * P], words[:, start + u : start + 2 * P : 2], ident[:]
+                    )
+                copy = nc.vector.tensor_copy if i == 1 else nc.scalar.copy
+                copy(
+                    out=grouped_words[:, i * ROW_WORDS : (i + 1) * ROW_WORDS].rearrange(
+                        "p (g r u) -> p g r u", g=D_PASSES, u=2
+                    ),
+                    in_=bank[:].rearrange("p (g u r) -> p g r u", g=D_PASSES, u=2),
+                )
+            nc.vector.quantize_mx(
+                out=codes[:].rearrange("p i g r -> p (i g r)").bitcast(FP8X4),
+                scales=scales[:].rearrange("p i g r -> p (i g r)"),
+                in_=grouped[:],
+            )
+
+        def project(weight, tokens, projected, leave_psum, b, h, first, count):
+            w_codes, w_scales = weight[h]
+            x_codes, x_scales = tokens[b]
+            codes, scales = projected
+            grouped = stage.tile([P, 2 * BANK], BF16, tag="grouped_tokens", align_bytes=64)
+            for n in range(count):
+                bank = psum.tile([P, BANK], F32, tag="bank")
+                for t in range(PACK):
+                    for g in range(D_PASSES):
+                        nc.tensor.matmul_mx(
+                            out=bank[:, t * P : (t + 1) * P],
+                            lhsT=w_codes[:, t, g, :].bitcast(FP8X4),
+                            lhsT_scale=w_scales[:, t, g, :],
+                            rhs=x_codes[:, first + n, g, :].bitcast(FP8X4),
+                            rhs_scale=x_scales[:, first + n, g, :],
+                            start=(g == 0),
+                            stop=(g == D_PASSES - 1),
+                        )
+                leave_psum(
+                    out=grouped[:, n * BANK : (n + 1) * BANK].rearrange("p (r t) -> p r t", t=PACK),
+                    in_=bank[:].rearrange("p (t r) -> p r t", t=PACK),
+                )
+            nc.vector.quantize_mx(
+                out=codes[:, b, h, first * P : (first + count) * P].bitcast(FP8X4),
+                scales=scales[:, b, h, first * P : (first + count) * P],
+                in_=grouped[:, 0 : count * BANK],
+            )
+
+        def project_keys(b, h, first, count):
+            project(ent, k_tok, k_mx, nc.scalar.copy, b, h, first, count)
+
+        def copy_scaled(out, in_):
+            nc.scalar.mul(out=out, in_=in_, mul=SCORE_SCALE)
+
+        def project_query_tile(n):
+            for h in range(DR_PASSES):
+                project(rot, q_tok, q_mx, copy_scaled, n // TILES, h, n % TILES, 1)
+
+        masked = [None] * QUERY_TILES
+        neg_max = [None] * QUERY_TILES
+        expd = [None] * QUERY_TILES
+        row_sum = [None] * QUERY_TILES
+        inverse = [None] * QUERY_TILES
+
+        def scores(n):
+            b, j = n // TILES, n % TILES
+            q_codes, q_scales = q_mx
+            k_codes, k_scales = k_mx
+            bank = psum.tile([P, BANK], F32, tag="bank")
+            for h in range(DR_PASSES):
+                nc.tensor.matmul_mx(
+                    out=bank[:],
+                    lhsT=q_codes[:, b, h, j * P : (j + 1) * P].bitcast(FP8X4),
+                    lhsT_scale=q_scales[:, b, h, j * P : (j + 1) * P],
+                    rhs=k_codes[:, b, h, :].bitcast(FP8X4),
+                    rhs_scale=k_scales[:, b, h, :],
+                    start=(h == 0),
+                    stop=(h == DR_PASSES - 1),
+                )
+            return bank
+
+        def mask_scores(n, bank):
+            masked[n] = soft.tile([P, S], F32, name="masked%d" % n, tag="masked")
+            nc.vector.scalar_tensor_tensor(
+                out=masked[n][:],
+                in0=mask_words[:, n % TILES, 0 : 2 * S : 2],
+                scalar=-FAR,
+                in1=bank[:],
+                op0=ALU.mult,
+                op1=ALU.add,
+            )
+
+        def row_maximum(n):
+            neg_max[n] = small.tile([P, 1], F32, name="neg_max%d" % n, tag="neg_max")
+            nc.vector.tensor_reduce(out=neg_max[n][:], in_=masked[n][:], axis=AXIS.X, op=ALU.max, negate=True)
+
+        def exponentials(n):
+            expd[n] = soft.tile([P, S], F32, name="expd%d" % n, tag="expd")
+            row_sum[n] = small.tile([P, 1], F32, name="row_sum%d" % n, tag="row_sum")
+            nc.scalar.activation(
+                out=expd[n][:],
+                in_=masked[n][:],
+                func=ACT.Exp,
+                bias=neg_max[n][:],
+                scale=1.0,
+                accum_out=row_sum[n][:],
+            )
+
+        def invert_row_sum(n):
+            inverse[n] = small.tile([P, 1], F32, name="inverse%d" % n, tag="inverse")
+            nc.vector.reciprocal(out=inverse[n][:], in_=row_sum[n][:])
+
+        def normalise_and_store(n):
+            weights = soft.tile([P, S], F32, tag="weights")
+            nc.vector.tensor_scalar_mul(out=weights[:], in0=expd[n][:], scalar1=inverse[n][:])
+            nc.sync.dma_start(out=out[n // TILES, (n % TILES) * P : (n % TILES + 1) * P, :], in_=weights[:])
+
+        quantise_chunk(ent_rows[0], ent[0])
+        quantise_chunk(k_rows[0], k_tok[0])
+        quantise_chunk(ent_rows[1], ent[1])
+        project_keys(0, 0, 0, 2)
+        quantise_chunk(rot_rows[0], rot[0])
+        project_keys(0, 0, 2, 2)
+        quantise_chunk(rot_rows[1], rot[1])
+        project_keys(0, 1, 0, 2)
+        quantise_chunk(q_rows[0], q_tok[0])
+        project_keys(0, 1, 2, 2)
+        quantise_chunk(k_rows[1], k_tok[1])
+        for n in range(AHEAD):
+            project_query_tile(n)
+        quantise_chunk(q_rows[1], q_tok[1])
+
+        for n in range(QUERY_TILES + 1):
+            if n < QUERY_TILES:
+                bank = scores(n)
+            if n >= 1:
+                exponentials(n - 1)
+            if n < QUERY_TILES:
+                mask_scores(n, bank)
+            if n >= 1:
+                invert_row_sum(n - 1)
+            if n < QUERY_TILES:
+                row_maximum(n)
+            if n >= 1:
+                normalise_and_store(n - 1)
+            if n < TILES:
+                project_keys(1, n // 2, 2 * (n % 2), 2)
+            if n + AHEAD < QUERY_TILES:
+                project_query_tile(n + AHEAD)

@@ -36,6 +36,7 @@ def tile_selfattention_pa_kernel(tc, q_lin, k_lin, rotation_params, entangle_par
     with ExitStack() as ctx:
         keep = ctx.enter_context(tc.tile_pool(name="keep", bufs=1))
         stage = ctx.enter_context(tc.tile_pool(name="stage", bufs=3))
+        rows_pool = ctx.enter_context(tc.tile_pool(name="rows", bufs=12))
         soft = ctx.enter_context(tc.tile_pool(name="soft", bufs=3))
         small = ctx.enter_context(tc.tile_pool(name="small", bufs=4))
         psum = ctx.enter_context(tc.psum_pool(name="psum", bufs=8))
@@ -89,30 +90,46 @@ def tile_selfattention_pa_kernel(tc, q_lin, k_lin, rotation_params, entangle_par
         k_mx = new_operand("k", [B, DR_PASSES, S])
         q_mx = new_operand("q", [B, DR_PASSES, S])
 
-        def quantise_chunk(chunk, operand):
-            codes, scales = operand
-            words = chunk[:].bitcast(F32)
-            grouped = stage.tile([P, TILES * D], BF16, tag="grouped_rows", align_bytes=64)
-            grouped_words = grouped[:].bitcast(F32)
-            for i in range(TILES):
+        def split_rows(chunk, tiles):
+            split = {}
+            for i in tiles:
+                split[i] = rows_pool.tile([P, D], BF16, name="split", tag="split")
+                nc.vector.tensor_copy(
+                    out=split[i][:].bitcast(F32).rearrange("p (u w) -> p u w", u=2),
+                    in_=chunk[:].bitcast(F32)[:, i * ROW_WORDS : (i + 1) * ROW_WORDS].rearrange("p (w u) -> p u w", u=2),
+                )
+            return split
+
+        def new_grouped():
+            grouped = stage.tile([P, TILES * D], BF16, name="grouped_rows", tag="grouped_rows", align_bytes=64)
+            return grouped
+
+        def turn(chunk, split, grouped, tiles, by_vector):
+            half = ROW_WORDS // 2
+            for i in tiles:
                 bank = psum.tile([P, BANK], F32, tag="bank")
                 for c in range(ROW_WORDS // P):
                     g, u = c // 2, c % 2
-                    start = i * ROW_WORDS + g * 2 * P
-                    nc.tensor.transpose(
-                        bank[:, c * P : (c + 1) * P], words[:, start + u : start + 2 * P : 2], ident[:]
-                    )
-                copy = nc.vector.tensor_copy if i == 1 else nc.scalar.copy
+                    if i in split:
+                        rows = split[i][:].bitcast(F32)[:, u * half + g * P : u * half + (g + 1) * P]
+                    else:
+                        start = i * ROW_WORDS + g * 2 * P
+                        rows = chunk[:].bitcast(F32)[:, start + u : start + 2 * P : 2]
+                    nc.tensor.transpose(bank[:, c * P : (c + 1) * P], rows, ident[:])
+                copy = nc.vector.tensor_copy if i in by_vector else nc.scalar.copy
                 copy(
-                    out=grouped_words[:, i * ROW_WORDS : (i + 1) * ROW_WORDS].rearrange(
+                    out=grouped[:].bitcast(F32)[:, i * ROW_WORDS : (i + 1) * ROW_WORDS].rearrange(
                         "p (g r u) -> p g r u", g=D_PASSES, u=2
                     ),
                     in_=bank[:].rearrange("p (g u r) -> p g r u", g=D_PASSES, u=2),
                 )
+
+        def quantise(grouped, operand, first, count):
+            codes, scales = operand
             nc.vector.quantize_mx(
-                out=codes[:].rearrange("p i g r -> p (i g r)").bitcast(FP8X4),
-                scales=scales[:].rearrange("p i g r -> p (i g r)"),
-                in_=grouped[:],
+                out=codes[:, first : first + count, :, :].rearrange("p i g r -> p (i g r)").bitcast(FP8X4),
+                scales=scales[:, first : first + count, :, :].rearrange("p i g r -> p (i g r)"),
+                in_=grouped[:, first * D : (first + count) * D],
             )
 
         def project(weight, tokens, projected, leave_psum, b, h, first, count):
@@ -212,20 +229,50 @@ def tile_selfattention_pa_kernel(tc, q_lin, k_lin, rotation_params, entangle_par
             nc.vector.tensor_scalar_mul(out=weights[:], in0=expd[n][:], scalar1=inverse[n][:])
             nc.sync.dma_start(out=out[n // TILES, (n % TILES) * P : (n % TILES + 1) * P, :], in_=weights[:])
 
-        quantise_chunk(ent_rows[0], ent[0])
-        quantise_chunk(k_rows[0], k_tok[0])
-        quantise_chunk(ent_rows[1], ent[1])
+        nosplit = {}
+        all4 = range(TILES)
+        g = new_grouped()
+        turn(ent_rows[0], nosplit, g, all4, (1,))
+        quantise(g, ent[0], 0, 4)
+        g = new_grouped()
+        turn(k_rows[0], nosplit, g, (0, 1), (1,))
+        quantise(g, k_tok[0], 0, 2)
+        turn(k_rows[0], nosplit, g, (2, 3), ())
+        quantise(g, k_tok[0], 2, 2)
+        g = new_grouped()
+        turn(ent_rows[1], nosplit, g, all4, (1,))
+        s = split_rows(rot_rows[0], (0, 1, 2))
+        quantise(g, ent[1], 0, 4)
         project_keys(0, 0, 0, 2)
-        quantise_chunk(rot_rows[0], rot[0])
+
+        g = new_grouped()
+        turn(rot_rows[0], s, g, all4, (1,))
+        s = split_rows(rot_rows[1], (0, 1, 2))
+        quantise(g, rot[0], 0, 4)
         project_keys(0, 0, 2, 2)
-        quantise_chunk(rot_rows[1], rot[1])
+
+        g = new_grouped()
+        turn(rot_rows[1], s, g, all4, (1,))
+        s = split_rows(q_rows[0], (0, 1, 2))
+        quantise(g, rot[1], 0, 4)
         project_keys(0, 1, 0, 2)
-        quantise_chunk(q_rows[0], q_tok[0])
+
+        g = new_grouped()
+        turn(q_rows[0], s, g, all4, (1,))
+        s = split_rows(k_rows[1], (0, 1, 2))
+        quantise(g, q_tok[0], 0, 4)
         project_keys(0, 1, 2, 2)
-        quantise_chunk(k_rows[1], k_tok[1])
-        for n in range(AHEAD):
-            project_query_tile(n)
-        quantise_chunk(q_rows[1], q_tok[1])
+
+        g = new_grouped()
+        turn(k_rows[1], s, g, all4, (1,))
+        s = split_rows(q_rows[1], (0, 1, 2))
+        quantise(g, k_tok[1], 0, 4)
+        project_query_tile(0)
+        project_query_tile(1)
+
+        g = new_grouped()
+        turn(q_rows[1], s, g, all4, (1,))
+        quantise(g, q_tok[1], 0, 4)
 
         for n in range(QUERY_TILES + 1):
             if n < QUERY_TILES:

@@ -61,11 +61,12 @@ def tile_selfattention_pa_kernel(tc, q_lin, k_lin, rotation_params, entangle_par
         ent_rows[0] = load_chunk("ent_rows0", weight_rows(entangle_params, 0))
         k_rows[0] = load_chunk("k_rows0", token_rows(k_lin, 0))
         ent_rows[1] = load_chunk("ent_rows1", weight_rows(entangle_params, 1))
+        k_rows[1] = load_chunk("k_rows1", token_rows(k_lin, 1))
         rot_rows[0] = load_chunk("rot_rows0", weight_rows(rotation_params, 0))
         rot_rows[1] = load_chunk("rot_rows1", weight_rows(rotation_params, 1))
         q_rows[0] = load_chunk("q_rows0", token_rows(q_lin, 0))
-        k_rows[1] = load_chunk("k_rows1", token_rows(k_lin, 1))
         q_rows[1] = load_chunk("q_rows1", token_rows(q_lin, 1))
+        rows = {"E0": ent_rows[0], "E1": ent_rows[1], "R0": rot_rows[0], "R1": rot_rows[1], "K0": k_rows[0], "K1": k_rows[1], "Q0": q_rows[0], "Q1": q_rows[1]}
         mask_words = keep.tile([P, TILES, 2 * S], I32, name="mask_words")
         for j in range(TILES):
             nc.sync.dma_start(out=mask_words[:, j, :], in_=mask.bitcast(I32)[j * P : (j + 1) * P, :])
@@ -90,53 +91,52 @@ def tile_selfattention_pa_kernel(tc, q_lin, k_lin, rotation_params, entangle_par
         k_mx = new_operand("k", [B, DR_PASSES, S])
         q_mx = new_operand("q", [B, DR_PASSES, S])
 
-        def split_rows(chunk, tiles):
-            split = {}
-            for i in tiles:
-                split[i] = rows_pool.tile([P, D], BF16, name="split", tag="split")
-                nc.vector.tensor_copy(
-                    out=split[i][:].bitcast(F32).rearrange("p (u w) -> p u w", u=2),
-                    in_=chunk[:].bitcast(F32)[:, i * ROW_WORDS : (i + 1) * ROW_WORDS].rearrange("p (w u) -> p u w", u=2),
-                )
-            return split
+        operands = {"E0": ent[0], "E1": ent[1], "R0": rot[0], "R1": rot[1], "K0": k_tok[0], "K1": k_tok[1], "Q0": q_tok[0], "Q1": q_tok[1]}
+        grouped_rows = {}
+        split = {}
 
-        def new_grouped():
-            grouped = stage.tile([P, TILES * D], BF16, name="grouped_rows", tag="grouped_rows", align_bytes=64)
-            return grouped
+        def split_row(name, i):
+            chunk = rows[name]
+            split[name, i] = rows_pool.tile([P, D], BF16, name="split", tag="split")
+            nc.vector.tensor_copy(
+                out=split[name, i][:].bitcast(F32).rearrange("p (u w) -> p u w", u=2),
+                in_=chunk[:].bitcast(F32)[:, i * ROW_WORDS : (i + 1) * ROW_WORDS].rearrange("p (w u) -> p u w", u=2),
+            )
 
-        def turn(chunk, split, grouped, tiles, by_vector):
+        def turn(name, i, leave_psum):
             half = ROW_WORDS // 2
-            for i in tiles:
-                bank = psum.tile([P, BANK], F32, tag="bank")
-                for c in range(ROW_WORDS // P):
-                    g, u = c // 2, c % 2
-                    if i in split:
-                        rows = split[i][:].bitcast(F32)[:, u * half + g * P : u * half + (g + 1) * P]
-                    else:
-                        start = i * ROW_WORDS + g * 2 * P
-                        rows = chunk[:].bitcast(F32)[:, start + u : start + 2 * P : 2]
-                    nc.tensor.transpose(bank[:, c * P : (c + 1) * P], rows, ident[:])
-                copy = nc.vector.tensor_copy if i in by_vector else nc.scalar.copy
-                copy(
-                    out=grouped[:].bitcast(F32)[:, i * ROW_WORDS : (i + 1) * ROW_WORDS].rearrange(
-                        "p (g r u) -> p g r u", g=D_PASSES, u=2
-                    ),
-                    in_=bank[:].rearrange("p (g u r) -> p g r u", g=D_PASSES, u=2),
-                )
+            if name not in grouped_rows:
+                grouped_rows[name] = stage.tile([P, TILES * D], BF16, name="grouped_rows", tag="grouped_rows", align_bytes=64)
+            bank = psum.tile([P, BANK], F32, tag="bank")
+            for c in range(ROW_WORDS // P):
+                g, u = c // 2, c % 2
+                if (name, i) in split:
+                    words = split[name, i][:].bitcast(F32)[:, u * half + g * P : u * half + (g + 1) * P]
+                else:
+                    start = i * ROW_WORDS + g * 2 * P
+                    words = rows[name][:].bitcast(F32)[:, start + u : start + 2 * P : 2]
+                nc.tensor.transpose(bank[:, c * P : (c + 1) * P], words, ident[:])
+            leave_psum(
+                out=grouped_rows[name][:].bitcast(F32)[:, i * ROW_WORDS : (i + 1) * ROW_WORDS].rearrange(
+                    "p (g r u) -> p g r u", g=D_PASSES, u=2
+                ),
+                in_=bank[:].rearrange("p (g u r) -> p g r u", g=D_PASSES, u=2),
+            )
 
-        def quantise(grouped, operand, first, count):
-            codes, scales = operand
+        def quantise(name, first, count):
+            codes, scales = operands[name]
             nc.vector.quantize_mx(
                 out=codes[:, first : first + count, :, :].rearrange("p i g r -> p (i g r)").bitcast(FP8X4),
                 scales=scales[:, first : first + count, :, :].rearrange("p i g r -> p (i g r)"),
-                in_=grouped[:, first * D : (first + count) * D],
+                in_=grouped_rows[name][:, first * D : (first + count) * D],
             )
+
+        pending = []
 
         def project(weight, tokens, projected, leave_psum, b, h, first, count):
             w_codes, w_scales = weight[h]
             x_codes, x_scales = tokens[b]
-            codes, scales = projected
-            grouped = stage.tile([P, 2 * BANK], BF16, tag="grouped_tokens", align_bytes=64)
+            grouped = stage.tile([P, 2 * BANK], BF16, name="grouped_tokens", tag="grouped_tokens", align_bytes=64)
             for n in range(count):
                 bank = psum.tile([P, BANK], F32, tag="bank")
                 for t in range(PACK):
@@ -154,6 +154,11 @@ def tile_selfattention_pa_kernel(tc, q_lin, k_lin, rotation_params, entangle_par
                     out=grouped[:, n * BANK : (n + 1) * BANK].rearrange("p (r t) -> p r t", t=PACK),
                     in_=bank[:].rearrange("p (t r) -> p r t", t=PACK),
                 )
+            pending.append((projected, grouped, b, h, first, count))
+
+        def quantise_projected():
+            projected, grouped, b, h, first, count = pending.pop(0)
+            codes, scales = projected
             nc.vector.quantize_mx(
                 out=codes[:, b, h, first * P : (first + count) * P].bitcast(FP8X4),
                 scales=scales[:, b, h, first * P : (first + count) * P],
@@ -166,9 +171,8 @@ def tile_selfattention_pa_kernel(tc, q_lin, k_lin, rotation_params, entangle_par
         def copy_scaled(out, in_):
             nc.scalar.mul(out=out, in_=in_, mul=SCORE_SCALE)
 
-        def project_query_tile(n):
-            for h in range(DR_PASSES):
-                project(rot, q_tok, q_mx, copy_scaled, n // TILES, h, n % TILES, 1)
+        def project_query(n, h):
+            project(rot, q_tok, q_mx, copy_scaled, n // TILES, h, n % TILES, 1)
 
         masked = [None] * QUERY_TILES
         neg_max = [None] * QUERY_TILES
@@ -224,70 +228,184 @@ def tile_selfattention_pa_kernel(tc, q_lin, k_lin, rotation_params, entangle_par
             inverse[n] = small.tile([P, 1], F32, name="inverse%d" % n, tag="inverse")
             nc.vector.reciprocal(out=inverse[n][:], in_=row_sum[n][:])
 
-        def normalise_and_store(n):
+        def normalise_and_store(n, by_gpsimd=False):
             weights = soft.tile([P, S], F32, tag="weights")
-            nc.vector.tensor_scalar_mul(out=weights[:], in0=expd[n][:], scalar1=inverse[n][:])
-            nc.sync.dma_start(out=out[n // TILES, (n % TILES) * P : (n % TILES + 1) * P, :], in_=weights[:])
+            rows_out = out[n // TILES, (n % TILES) * P : (n % TILES + 1) * P, :]
+            if n == QUERY_TILES - 1:
+                for half in (slice(0, S // 2), slice(S // 2, S)):
+                    nc.vector.tensor_scalar_mul(out=weights[:, half], in0=expd[n][:, half], scalar1=inverse[n][:])
+                    nc.sync.dma_start(out=rows_out[:, half], in_=weights[:, half])
+                return
+            if by_gpsimd:
+                nc.gpsimd.tensor_scalar(
+                    out=weights[:], in0=expd[n][:], scalar1=inverse[n][:], scalar2=0.0, op0=ALU.mult, op1=ALU.add
+                )
+            else:
+                nc.vector.tensor_scalar_mul(out=weights[:], in0=expd[n][:], scalar1=inverse[n][:])
+            nc.sync.dma_start(out=rows_out, in_=weights[:])
 
-        nosplit = {}
-        all4 = range(TILES)
-        g = new_grouped()
-        turn(ent_rows[0], nosplit, g, all4, (1,))
-        quantise(g, ent[0], 0, 4)
-        g = new_grouped()
-        turn(k_rows[0], nosplit, g, (0, 1), (1,))
-        quantise(g, k_tok[0], 0, 2)
-        turn(k_rows[0], nosplit, g, (2, 3), ())
-        quantise(g, k_tok[0], 2, 2)
-        g = new_grouped()
-        turn(ent_rows[1], nosplit, g, all4, (1,))
-        s = split_rows(rot_rows[0], (0, 1, 2))
-        quantise(g, ent[1], 0, 4)
-        project_keys(0, 0, 0, 2)
-
-        g = new_grouped()
-        turn(rot_rows[0], s, g, all4, (1,))
-        s = split_rows(rot_rows[1], (0, 1, 2))
-        quantise(g, rot[0], 0, 4)
+        turn("E0", 0, nc.scalar.copy)
+        turn("E0", 1, nc.vector.tensor_copy)
+        turn("E0", 2, nc.scalar.copy)
+        turn("E0", 3, nc.scalar.copy)
+        quantise("E0", 0, 2)
+        quantise("E0", 2, 2)
+        turn("K0", 0, nc.scalar.copy)
+        quantise("K0", 0, 1)
+        turn("K0", 1, nc.scalar.copy)
+        quantise("K0", 1, 1)
+        turn("K0", 2, nc.scalar.copy)
+        split_row("E1", 0)
+        turn("K0", 3, nc.vector.tensor_copy)
+        project_keys(0, 0, 0, 1)
+        project_keys(0, 0, 1, 1)
+        split_row("E1", 1)
+        split_row("E1", 2)
+        quantise("K0", 2, 2)
+        split_row("E1", 3)
+        turn("E1", 0, nc.scalar.copy)
+        quantise_projected()
+        quantise_projected()
+        split_row("K1", 0)
+        split_row("K1", 1)
+        turn("E1", 1, nc.vector.tensor_copy)
+        turn("E1", 2, nc.scalar.copy)
+        turn("E1", 3, nc.scalar.copy)
+        split_row("K1", 2)
+        split_row("K1", 3)
+        quantise("E1", 0, 4)
         project_keys(0, 0, 2, 2)
-
-        g = new_grouped()
-        turn(rot_rows[1], s, g, all4, (1,))
-        s = split_rows(q_rows[0], (0, 1, 2))
-        quantise(g, rot[1], 0, 4)
+        turn("K1", 0, nc.scalar.copy)
+        turn("K1", 1, nc.vector.tensor_copy)
+        turn("K1", 2, nc.scalar.copy)
+        turn("K1", 3, nc.scalar.copy)
+        quantise_projected()
+        split_row("R0", 0)
+        split_row("R0", 1)
+        split_row("R0", 2)
+        split_row("R0", 3)
+        quantise("K1", 0, 4)
         project_keys(0, 1, 0, 2)
-
-        g = new_grouped()
-        turn(q_rows[0], s, g, all4, (1,))
-        s = split_rows(k_rows[1], (0, 1, 2))
-        quantise(g, q_tok[0], 0, 4)
+        quantise_projected()
+        turn("R0", 0, nc.scalar.copy)
+        turn("R0", 1, nc.vector.tensor_copy)
+        turn("R0", 2, nc.scalar.copy)
+        turn("R0", 3, nc.scalar.copy)
+        split_row("R1", 0)
+        split_row("R1", 1)
+        split_row("R1", 2)
+        split_row("R1", 3)
+        quantise("R0", 0, 4)
         project_keys(0, 1, 2, 2)
-
-        g = new_grouped()
-        turn(k_rows[1], s, g, all4, (1,))
-        s = split_rows(q_rows[1], (0, 1, 2))
-        quantise(g, k_tok[1], 0, 4)
-        project_query_tile(0)
-        project_query_tile(1)
-
-        g = new_grouped()
-        turn(q_rows[1], s, g, all4, (1,))
-        quantise(g, q_tok[1], 0, 4)
-
-        for n in range(QUERY_TILES + 1):
-            if n < QUERY_TILES:
-                bank = scores(n)
-            if n >= 1:
-                exponentials(n - 1)
-            if n < QUERY_TILES:
-                mask_scores(n, bank)
-            if n >= 1:
-                invert_row_sum(n - 1)
-            if n < QUERY_TILES:
-                row_maximum(n)
-            if n >= 1:
-                normalise_and_store(n - 1)
-            if n < TILES:
-                project_keys(1, n // 2, 2 * (n % 2), 2)
-            if n + AHEAD < QUERY_TILES:
-                project_query_tile(n + AHEAD)
+        quantise_projected()
+        turn("R1", 0, nc.scalar.copy)
+        turn("R1", 1, nc.vector.tensor_copy)
+        turn("R1", 2, nc.scalar.copy)
+        turn("R1", 3, nc.scalar.copy)
+        split_row("Q0", 0)
+        split_row("Q0", 1)
+        split_row("Q0", 2)
+        split_row("Q0", 3)
+        quantise("R1", 0, 4)
+        project_keys(1, 0, 0, 2)
+        quantise_projected()
+        project_keys(1, 0, 2, 2)
+        quantise_projected()
+        turn("Q0", 0, nc.scalar.copy)
+        turn("Q0", 1, nc.vector.tensor_copy)
+        turn("Q0", 2, nc.scalar.copy)
+        turn("Q0", 3, nc.scalar.copy)
+        split_row("Q1", 0)
+        split_row("Q1", 1)
+        split_row("Q1", 2)
+        split_row("Q1", 3)
+        quantise("Q0", 0, 4)
+        project_keys(1, 1, 0, 2)
+        quantise_projected()
+        project_keys(1, 1, 2, 2)
+        quantise_projected()
+        turn("Q1", 0, nc.scalar.copy)
+        turn("Q1", 1, nc.vector.tensor_copy)
+        turn("Q1", 2, nc.scalar.copy)
+        turn("Q1", 3, nc.scalar.copy)
+        quantise("Q1", 0, 4)
+        project_query(0, 0)
+        quantise_projected()
+        project_query(0, 1)
+        quantise_projected()
+        project_query(1, 0)
+        quantise_projected()
+        project_query(1, 1)
+        quantise_projected()
+        bank0 = scores(0)
+        mask_scores(0, bank0)
+        row_maximum(0)
+        project_query(2, 0)
+        quantise_projected()
+        project_query(2, 1)
+        bank1 = scores(1)
+        exponentials(0)
+        mask_scores(1, bank1)
+        quantise_projected()
+        row_maximum(1)
+        invert_row_sum(0)
+        normalise_and_store(0, True)
+        project_query(3, 0)
+        quantise_projected()
+        project_query(3, 1)
+        bank2 = scores(2)
+        exponentials(1)
+        mask_scores(2, bank2)
+        quantise_projected()
+        row_maximum(2)
+        invert_row_sum(1)
+        normalise_and_store(1, True)
+        project_query(4, 0)
+        quantise_projected()
+        project_query(4, 1)
+        bank3 = scores(3)
+        exponentials(2)
+        mask_scores(3, bank3)
+        quantise_projected()
+        row_maximum(3)
+        invert_row_sum(2)
+        normalise_and_store(2, True)
+        project_query(5, 0)
+        quantise_projected()
+        project_query(5, 1)
+        bank4 = scores(4)
+        exponentials(3)
+        mask_scores(4, bank4)
+        quantise_projected()
+        row_maximum(4)
+        invert_row_sum(3)
+        normalise_and_store(3, True)
+        project_query(6, 0)
+        quantise_projected()
+        project_query(6, 1)
+        bank5 = scores(5)
+        exponentials(4)
+        mask_scores(5, bank5)
+        quantise_projected()
+        row_maximum(5)
+        invert_row_sum(4)
+        normalise_and_store(4, True)
+        project_query(7, 0)
+        quantise_projected()
+        project_query(7, 1)
+        bank6 = scores(6)
+        exponentials(5)
+        mask_scores(6, bank6)
+        quantise_projected()
+        row_maximum(6)
+        invert_row_sum(5)
+        normalise_and_store(5, True)
+        bank7 = scores(7)
+        exponentials(6)
+        mask_scores(7, bank7)
+        row_maximum(7)
+        invert_row_sum(6)
+        normalise_and_store(6, True)
+        exponentials(7)
+        invert_row_sum(7)
+        normalise_and_store(7, False)

@@ -91,6 +91,13 @@ def tile_selfattention_pa_kernel(tc, q_lin, k_lin, rotation_params, entangle_par
         k_mx = new_operand("k", [B, DR_PASSES, S])
         q_mx = new_operand("q", [B, DR_PASSES, S])
 
+        warm = keep.tile([P, BANK], BF16, name="warm")
+        nc.vector.memset(warm[:], 0.0)
+
+        def warm_up():
+            bank = psum.tile([P, BANK], F32, tag="bank")
+            nc.tensor.matmul(bank[:], lhsT=warm[:, 0:P], rhs=warm[:], start=True, stop=True)
+
         operands = {"E0": ent[0], "E1": ent[1], "R0": rot[0], "R1": rot[1], "K0": k_tok[0], "K1": k_tok[1], "Q0": q_tok[0], "Q1": q_tok[1]}
         grouped_rows = {}
         split = {}
@@ -244,6 +251,10 @@ def tile_selfattention_pa_kernel(tc, q_lin, k_lin, rotation_params, entangle_par
                 nc.vector.tensor_scalar_mul(out=weights[:], in0=expd[n][:], scalar1=inverse[n][:])
             nc.sync.dma_start(out=rows_out, in_=weights[:])
 
+        warm_up()
+        warm_up()
+        warm_up()
+        warm_up()
         turn("E0", 0, nc.scalar.copy)
         turn("E0", 1, nc.vector.tensor_copy)
         turn("E0", 2, nc.scalar.copy)
@@ -254,31 +265,37 @@ def tile_selfattention_pa_kernel(tc, q_lin, k_lin, rotation_params, entangle_par
         quantise("K0", 0, 1)
         turn("K0", 1, nc.scalar.copy)
         quantise("K0", 1, 1)
+        warm_up()
+        warm_up()
         turn("K0", 2, nc.scalar.copy)
-        split_row("E1", 0)
-        turn("K0", 3, nc.vector.tensor_copy)
+        split_row("K0", 3)
         project_keys(0, 0, 0, 1)
         project_keys(0, 0, 1, 1)
+        split_row("E1", 0)
         split_row("E1", 1)
+        quantise("K0", 2, 1)
         split_row("E1", 2)
-        quantise("K0", 2, 2)
         split_row("E1", 3)
-        turn("E1", 0, nc.scalar.copy)
-        quantise_projected()
+        turn("K0", 3, nc.scalar.copy)
+        turn("E1", 0, nc.vector.tensor_copy)
         quantise_projected()
         split_row("K1", 0)
+        quantise_projected()
+        quantise("K0", 3, 1)
         split_row("K1", 1)
-        turn("E1", 1, nc.vector.tensor_copy)
+        turn("E1", 1, nc.scalar.copy)
         turn("E1", 2, nc.scalar.copy)
         turn("E1", 3, nc.scalar.copy)
         split_row("K1", 2)
         split_row("K1", 3)
         quantise("E1", 0, 4)
-        project_keys(0, 0, 2, 2)
+        project_keys(0, 0, 2, 1)
+        project_keys(0, 0, 3, 1)
         turn("K1", 0, nc.scalar.copy)
         turn("K1", 1, nc.vector.tensor_copy)
         turn("K1", 2, nc.scalar.copy)
         turn("K1", 3, nc.scalar.copy)
+        quantise_projected()
         quantise_projected()
         split_row("R0", 0)
         split_row("R0", 1)
@@ -405,7 +422,7 @@ def tile_selfattention_pa_kernel(tc, q_lin, k_lin, rotation_params, entangle_par
         mask_scores(7, bank7)
         row_maximum(7)
         invert_row_sum(6)
-        normalise_and_store(6, True)
+        normalise_and_store(6, False)
         exponentials(7)
         invert_row_sum(7)
         normalise_and_store(7, False)

@@ -80,8 +80,8 @@ def tile_selfattention_pa_kernel(tc, q_lin, k_lin, rotation_params, entangle_par
         nc.scalar.activation(out=one[:], in_=zero[:], func=ACT.Exp)
 
         def new_operand(name, shape):
-            codes = keep.tile([P] + shape, U32, name=name + "_codes", align_bytes=64)
-            scales = keep.tile([P] + shape, U8, name=name + "_scales", align_bytes=64)
+            codes = keep.tile([P] + shape, U32, name=name + "_codes", align_bytes=256)
+            scales = keep.tile([P] + shape, U8, name=name + "_scales", align_bytes=256)
             return codes, scales
 
         ent = [new_operand("ent%d" % h, [TILES, D_PASSES, P]) for h in range(DR_PASSES)]
@@ -113,7 +113,7 @@ def tile_selfattention_pa_kernel(tc, q_lin, k_lin, rotation_params, entangle_par
         def turn(name, i, leave_psum):
             half = ROW_WORDS // 2
             if name not in grouped_rows:
-                grouped_rows[name] = stage.tile([P, TILES * D], BF16, name="grouped_rows", tag="grouped_rows", align_bytes=64)
+                grouped_rows[name] = stage.tile([P, TILES * D], BF16, name="grouped_rows", tag="grouped_rows", align_bytes=256)
             bank = psum.tile([P, BANK], F32, tag="bank")
             for c in range(ROW_WORDS // P):
                 g, u = c // 2, c % 2
@@ -143,7 +143,7 @@ def tile_selfattention_pa_kernel(tc, q_lin, k_lin, rotation_params, entangle_par
         def project(weight, tokens, projected, leave_psum, b, h, first, count):
             w_codes, w_scales = weight[h]
             x_codes, x_scales = tokens[b]
-            grouped = stage.tile([P, 2 * BANK], BF16, name="grouped_tokens", tag="grouped_tokens", align_bytes=64)
+            grouped = stage.tile([P, 2 * BANK], BF16, name="grouped_tokens", tag="grouped_tokens", align_bytes=256)
             for n in range(count):
                 bank = psum.tile([P, BANK], F32, tag="bank")
                 for t in range(PACK):
@@ -191,29 +191,36 @@ def tile_selfattention_pa_kernel(tc, q_lin, k_lin, rotation_params, entangle_par
             b, j = n // TILES, n % TILES
             q_codes, q_scales = q_mx
             k_codes, k_scales = k_mx
-            bank = psum.tile([P, BANK], F32, tag="bank")
+            parts = 2 if n == QUERY_TILES - 1 else 1
+            width = S // parts
+            banks = []
+            for i in range(parts):
+                bank = psum.tile([P, BANK], F32, name="bank", tag="bank")
+                banks.append((bank, slice(i * width, (i + 1) * width)))
             for h in range(DR_PASSES):
-                nc.tensor.matmul_mx(
-                    out=bank[:],
-                    lhsT=q_codes[:, b, h, j * P : (j + 1) * P].bitcast(FP8X4),
-                    lhsT_scale=q_scales[:, b, h, j * P : (j + 1) * P],
-                    rhs=k_codes[:, b, h, :].bitcast(FP8X4),
-                    rhs_scale=k_scales[:, b, h, :],
-                    start=(h == 0),
-                    stop=(h == DR_PASSES - 1),
-                )
-            return bank
+                for bank, keys in banks:
+                    nc.tensor.matmul_mx(
+                        out=bank[:, 0:width],
+                        lhsT=q_codes[:, b, h, j * P : (j + 1) * P].bitcast(FP8X4),
+                        lhsT_scale=q_scales[:, b, h, j * P : (j + 1) * P],
+                        rhs=k_codes[:, b, h, keys].bitcast(FP8X4),
+                        rhs_scale=k_scales[:, b, h, keys],
+                        start=(h == 0),
+                        stop=(h == DR_PASSES - 1),
+                    )
+            return banks
 
-        def mask_scores(n, bank):
+        def mask_scores(n, banks):
             masked[n] = soft.tile([P, S], F32, name="masked%d" % n, tag="masked")
-            nc.vector.scalar_tensor_tensor(
-                out=masked[n][:],
-                in0=mask_words[:, n % TILES, 0 : 2 * S : 2],
-                scalar=-FAR,
-                in1=bank[:],
-                op0=ALU.mult,
-                op1=ALU.add,
-            )
+            for bank, keys in banks:
+                nc.vector.scalar_tensor_tensor(
+                    out=masked[n][:, keys],
+                    in0=mask_words[:, n % TILES, 2 * keys.start : 2 * keys.stop : 2],
+                    scalar=-FAR,
+                    in1=bank[:, 0 : keys.stop - keys.start],
+                    op0=ALU.mult,
+                    op1=ALU.add,
+                )
 
         def row_maximum(n):
             neg_max[n] = small.tile([P, 1], F32, name="neg_max%d" % n, tag="neg_max")
@@ -315,6 +322,8 @@ def tile_selfattention_pa_kernel(tc, q_lin, k_lin, rotation_params, entangle_par
         quantise("R0", 0, 4)
         project_keys(0, 1, 2, 2)
         quantise_projected()
+        project_keys(1, 0, 0, 2)
+        quantise_projected()
         turn("R1", 0, nc.scalar.copy)
         turn("R1", 1, nc.vector.tensor_copy)
         turn("R1", 2, nc.scalar.copy)
@@ -324,9 +333,9 @@ def tile_selfattention_pa_kernel(tc, q_lin, k_lin, rotation_params, entangle_par
         split_row("Q0", 2)
         split_row("Q0", 3)
         quantise("R1", 0, 4)
-        project_keys(1, 0, 0, 2)
-        quantise_projected()
         project_keys(1, 0, 2, 2)
+        quantise_projected()
+        project_keys(1, 1, 0, 2)
         quantise_projected()
         turn("Q0", 0, nc.scalar.copy)
         turn("Q0", 1, nc.vector.tensor_copy)
@@ -337,8 +346,6 @@ def tile_selfattention_pa_kernel(tc, q_lin, k_lin, rotation_params, entangle_par
         split_row("Q1", 2)
         split_row("Q1", 3)
         quantise("Q0", 0, 4)
-        project_keys(1, 1, 0, 2)
-        quantise_projected()
         project_keys(1, 1, 2, 2)
         quantise_projected()
         turn("Q1", 0, nc.scalar.copy)

from contextlib import ExitStack

import concourse.mybir as mybir
from concourse.masks import make_identity

F32 = mybir.dt.float32
BF16 = mybir.dt.bfloat16
I32 = mybir.dt.int32
U32 = mybir.dt.uint32
U8 = mybir.dt.uint8
FP8X4 = mybir.dt.float8_e4m3fn_x4
ALU = mybir.AluOpType
ACT = mybir.ActivationFunctionType
AXIS = mybir.AxisListType

B, S, D, DR = 2, 512, 1024, 1024
P = 128
PACK = 4
K_PASS = P * PACK
BANK = 512
D_PASSES = D // K_PASS
DR_PASSES = DR // K_PASS
TILES = 4
ROW_WORDS = D // 2
QUERY_TILES = B * TILES
AHEAD = 2
FAR = 1.5e38
SCORE_SCALE = D**-0.5
assert SCORE_SCALE == 2.0**-5

FLOPS = 2 * (2 * B * S * D * DR) + 2 * B * S * S * DR


def tile_selfattention_pa_kernel(tc, q_lin, k_lin, rotation_params, entangle_params, mask, out):
    nc = tc.nc
    with ExitStack() as ctx:
        keep = ctx.enter_context(tc.tile_pool(name="keep", bufs=1))
        stage = ctx.enter_context(tc.tile_pool(name="stage", bufs=3))
        rows_pool = ctx.enter_context(tc.tile_pool(name="rows", bufs=12))
        soft = ctx.enter_context(tc.tile_pool(name="soft", bufs=3))
        small = ctx.enter_context(tc.tile_pool(name="small", bufs=4))
        psum = ctx.enter_context(tc.psum_pool(name="psum", bufs=8))
        ctx.enter_context(tc.manual_schedule())

        def load_chunk(name, rows_of_partition):
            chunk = keep.tile([P, TILES * D], BF16, name=name)
            for i in range(TILES):
                nc.sync.dma_start(out=chunk[:, i * D : (i + 1) * D], in_=rows_of_partition[:, i, :])
            return chunk

        def weight_rows(w, h):
            return w.rearrange("(h p i) d -> h p i d", h=DR_PASSES, i=TILES)[h]

        def token_rows(x, b):
            return x[b].rearrange("(i p) d -> p i d", p=P)

        ent_rows = [None] * DR_PASSES
        rot_rows = [None] * DR_PASSES
        k_rows = [None] * B
        q_rows = [None] * B
        ent_rows[0] = load_chunk("ent_rows0", weight_rows(entangle_params, 0))
        k_rows[0] = load_chunk("k_rows0", token_rows(k_lin, 0))
        ent_rows[1] = load_chunk("ent_rows1", weight_rows(entangle_params, 1))
        k_rows[1] = load_chunk("k_rows1", token_rows(k_lin, 1))
        rot_rows[0] = load_chunk("rot_rows0", weight_rows(rotation_params, 0))
        rot_rows[1] = load_chunk("rot_rows1", weight_rows(rotation_params, 1))
        q_rows[0] = load_chunk("q_rows0", token_rows(q_lin, 0))
        q_rows[1] = load_chunk("q_rows1", token_rows(q_lin, 1))
        rows = {"E0": ent_rows[0], "E1": ent_rows[1], "R0": rot_rows[0], "R1": rot_rows[1], "K0": k_rows[0], "K1": k_rows[1], "Q0": q_rows[0], "Q1": q_rows[1]}
        mask_words = keep.tile([P, TILES, 2 * S], I32, name="mask_words")
        for j in range(TILES):
            nc.sync.dma_start(out=mask_words[:, j, :], in_=mask.bitcast(I32)[j * P : (j + 1) * P, :])

        ident = keep.tile([P, P], F32, name="ident")
        make_identity(nc, ident[:])

        zero = small.tile([P, 1], F32, name="zero")
        one = small.tile([P, 1], F32, name="one")
        nc.vector.memset(zero[:], 0.0)
        nc.scalar.activation(out=one[:], in_=zero[:], func=ACT.Exp)

        def new_operand(name, shape):
            codes = keep.tile([P] + shape, U32, name=name + "_codes", align_bytes=256)
            scales = keep.tile([P] + shape, U8, name=name + "_scales", align_bytes=256)
            return codes, scales

        ent = [new_operand("ent%d" % h, [TILES, D_PASSES, P]) for h in range(DR_PASSES)]
        rot = [new_operand("rot%d" % h, [TILES, D_PASSES, P]) for h in range(DR_PASSES)]
        k_tok = [new_operand("k_tok%d" % b, [TILES, D_PASSES, P]) for b in range(B)]
        q_tok = [new_operand("q_tok%d" % b, [TILES, D_PASSES, P]) for b in range(B)]
        k_mx = new_operand("k", [B, DR_PASSES, S])
        q_mx = new_operand("q", [B, DR_PASSES, S])

        warm = keep.tile([P, BANK], BF16, name="warm")
        nc.vector.memset(warm[:], 0.0)

        def warm_up():
            bank = psum.tile([P, BANK], F32, tag="bank")
            nc.tensor.matmul(bank[:], lhsT=warm[:, 0:P], rhs=warm[:], start=True, stop=True)

        operands = {"E0": ent[0], "E1": ent[1], "R0": rot[0], "R1": rot[1], "K0": k_tok[0], "K1": k_tok[1], "Q0": q_tok[0], "Q1": q_tok[1]}
        grouped_rows = {}
        split = {}

        def split_row(name, i):
            chunk = rows[name]
            split[name, i] = rows_pool.tile([P, D], BF16, name="split", tag="split")
            nc.vector.tensor_copy(
                out=split[name, i][:].bitcast(F32).rearrange("p (u w) -> p u w", u=2),
                in_=chunk[:].bitcast(F32)[:, i * ROW_WORDS : (i + 1) * ROW_WORDS].rearrange("p (w u) -> p u w", u=2),
            )

        def turn(name, i, leave_psum):
            half = ROW_WORDS // 2
            if name not in grouped_rows:
                grouped_rows[name] = stage.tile([P, TILES * D], BF16, name="grouped_rows", tag="grouped_rows", align_bytes=256)
            bank = psum.tile([P, BANK], F32, tag="bank")
            for c in range(ROW_WORDS // P):
                g, u = c // 2, c % 2
                if (name, i) in split:
                    words = split[name, i][:].bitcast(F32)[:, u * half + g * P : u * half + (g + 1) * P]
                else:
                    start = i * ROW_WORDS + g * 2 * P
                    words = rows[name][:].bitcast(F32)[:, start + u : start + 2 * P : 2]
                nc.tensor.transpose(bank[:, c * P : (c + 1) * P], words, ident[:])
            leave_psum(
                out=grouped_rows[name][:].bitcast(F32)[:, i * ROW_WORDS : (i + 1) * ROW_WORDS].rearrange(
                    "p (g r u) -> p g r u", g=D_PASSES, u=2
                ),
                in_=bank[:].rearrange("p (g u r) -> p g r u", g=D_PASSES, u=2),
            )

        def quantise(name, first, count):
            codes, scales = operands[name]
            nc.vector.quantize_mx(
                out=codes[:, first : first + count, :, :].rearrange("p i g r -> p (i g r)").bitcast(FP8X4),
                scales=scales[:, first : first + count, :, :].rearrange("p i g r -> p (i g r)"),
                in_=grouped_rows[name][:, first * D : (first + count) * D],
            )

        pending = []

        def project(weight, tokens, projected, leave_psum, b, h, first, count):
            w_codes, w_scales = weight[h]
            x_codes, x_scales = tokens[b]
            grouped = stage.tile([P, 2 * BANK], BF16, name="grouped_tokens", tag="grouped_tokens", align_bytes=256)
            for n in range(count):
                bank = psum.tile([P, BANK], F32, tag="bank")
                for t in range(PACK):
                    for g in range(D_PASSES):
                        nc.tensor.matmul_mx(
                            out=bank[:, t * P : (t + 1) * P],
                            lhsT=w_codes[:, t, g, :].bitcast(FP8X4),
                            lhsT_scale=w_scales[:, t, g, :],
                            rhs=x_codes[:, first + n, g, :].bitcast(FP8X4),
                            rhs_scale=x_scales[:, first + n, g, :],
                            start=(g == 0),
                            stop=(g == D_PASSES - 1),
                        )
                leave_psum(
                    out=grouped[:, n * BANK : (n + 1) * BANK].rearrange("p (r t) -> p r t", t=PACK),
                    in_=bank[:].rearrange("p (t r) -> p r t", t=PACK),
                )
            pending.append((projected, grouped, b, h, first, count))

        def quantise_projected():
            projected, grouped, b, h, first, count = pending.pop(0)
            codes, scales = projected
            nc.vector.quantize_mx(
                out=codes[:, b, h, first * P : (first + count) * P].bitcast(FP8X4),
                scales=scales[:, b, h, first * P : (first + count) * P],
                in_=grouped[:, 0 : count * BANK],
            )

        def project_keys(b, h, first, count):
            project(ent, k_tok, k_mx, nc.scalar.copy, b, h, first, count)

        def copy_scaled(out, in_):
            nc.scalar.mul(out=out, in_=in_, mul=SCORE_SCALE)

        def project_query(n, h):
            project(rot, q_tok, q_mx, copy_scaled, n // TILES, h, n % TILES, 1)

        masked = [None] * QUERY_TILES
        neg_max = [None] * QUERY_TILES
        expd = [None] * QUERY_TILES
        row_sum = [None] * QUERY_TILES
        inverse = [None] * QUERY_TILES

        def scores(n):
            b, j = n // TILES, n % TILES
            q_codes, q_scales = q_mx
            k_codes, k_scales = k_mx
            parts = 2 if n == QUERY_TILES - 1 else 1
            width = S // parts
            banks = []
            for i in range(parts):
                bank = psum.tile([P, BANK], F32, name="bank", tag="bank")
                banks.append((bank, slice(i * width, (i + 1) * width)))
            for h in range(DR_PASSES):
                for bank, keys in banks:
                    nc.tensor.matmul_mx(
                        out=bank[:, 0:width],
                        lhsT=q_codes[:, b, h, j * P : (j + 1) * P].bitcast(FP8X4),
                        lhsT_scale=q_scales[:, b, h, j * P : (j + 1) * P],
                        rhs=k_codes[:, b, h, keys].bitcast(FP8X4),
                        rhs_scale=k_scales[:, b, h, keys],
                        start=(h == 0),
                        stop=(h == DR_PASSES - 1),
                    )
            return banks

        def mask_scores(n, banks):
            masked[n] = soft.tile([P, S], F32, name="masked%d" % n, tag="masked")
            for bank, keys in banks:
                nc.vector.scalar_tensor_tensor(
                    out=masked[n][:, keys],
                    in0=mask_words[:, n % TILES, 2 * keys.start : 2 * keys.stop : 2],
                    scalar=-FAR,
                    in1=bank[:, 0 : keys.stop - keys.start],
                    op0=ALU.mult,
                    op1=ALU.add,
                )

        def row_maximum(n):
            neg_max[n] = small.tile([P, 1], F32, name="neg_max%d" % n, tag="neg_max")
            nc.vector.tensor_reduce(out=neg_max[n][:], in_=masked[n][:], axis=AXIS.X, op=ALU.max, negate=True)

        def exponentials(n):
            expd[n] = soft.tile([P, S], F32, name="expd%d" % n, tag="expd")
            row_sum[n] = small.tile([P, 1], F32, name="row_sum%d" % n, tag="row_sum")
            nc.scalar.activation(
                out=expd[n][:],
                in_=masked[n][:],
                func=ACT.Exp,
                bias=neg_max[n][:],
                scale=1.0,
                accum_out=row_sum[n][:],
            )

        def invert_row_sum(n):
            inverse[n] = small.tile([P, 1], F32, name="inverse%d" % n, tag="inverse")
            nc.vector.reciprocal(out=inverse[n][:], in_=row_sum[n][:])

        def normalise_and_store(n, by_gpsimd=False):
            weights = soft.tile([P, S], F32, tag="weights")
            rows_out = out[n // TILES, (n % TILES) * P : (n % TILES + 1) * P, :]
            if n == QUERY_TILES - 1:
                for half in (slice(0, S // 2), slice(S // 2, S)):
                    nc.vector.tensor_scalar_mul(out=weights[:, half], in0=expd[n][:, half], scalar1=inverse[n][:])
                    nc.sync.dma_start(out=rows_out[:, half], in_=weights[:, half])
                return
            if by_gpsimd:
                nc.gpsimd.tensor_scalar(
                    out=weights[:], in0=expd[n][:], scalar1=inverse[n][:], scalar2=0.0, op0=ALU.mult, op1=ALU.add
                )
            else:
                nc.vector.tensor_scalar_mul(out=weights[:], in0=expd[n][:], scalar1=inverse[n][:])
            nc.sync.dma_start(out=rows_out, in_=weights[:])

        warm_up()
        warm_up()
        warm_up()
        warm_up()
        turn("E0", 0, nc.scalar.copy)
        turn("E0", 1, nc.vector.tensor_copy)
        turn("E0", 2, nc.scalar.copy)
        turn("E0", 3, nc.scalar.copy)
        quantise("E0", 0, 2)
        quantise("E0", 2, 2)
        turn("K0", 0, nc.scalar.copy)
        quantise("K0", 0, 1)
        turn("K0", 1, nc.scalar.copy)
        quantise("K0", 1, 1)
        warm_up()
        warm_up()
        turn("K0", 2, nc.scalar.copy)
        split_row("K0", 3)
        project_keys(0, 0, 0, 1)
        project_keys(0, 0, 1, 1)
        split_row("E1", 0)
        split_row("E1", 1)
        quantise("K0", 2, 1)
        split_row("E1", 2)
        split_row("E1", 3)
        turn("K0", 3, nc.scalar.copy)
        turn("E1", 0, nc.vector.tensor_copy)
        quantise_projected()
        split_row("K1", 0)
        quantise_projected()
        quantise("K0", 3, 1)
        split_row("K1", 1)
        turn("E1", 1, nc.scalar.copy)
        turn("E1", 2, nc.scalar.copy)
        turn("E1", 3, nc.scalar.copy)
        split_row("K1", 2)
        split_row("K1", 3)
        quantise("E1", 0, 4)
        project_keys(0, 0, 2, 1)
        project_keys(0, 0, 3, 1)
        turn("K1", 0, nc.scalar.copy)
        turn("K1", 1, nc.vector.tensor_copy)
        turn("K1", 2, nc.scalar.copy)
        turn("K1", 3, nc.scalar.copy)
        quantise_projected()
        quantise_projected()
        split_row("R0", 0)
        split_row("R0", 1)
        split_row("R0", 2)
        split_row("R0", 3)
        quantise("K1", 0, 4)
        project_keys(0, 1, 0, 2)
        quantise_projected()
        turn("R0", 0, nc.scalar.copy)
        turn("R0", 1, nc.vector.tensor_copy)
        turn("R0", 2, nc.scalar.copy)
        turn("R0", 3, nc.scalar.copy)
        split_row("R1", 0)
        split_row("R1", 1)
        split_row("R1", 2)
        split_row("R1", 3)
        quantise("R0", 0, 4)
        project_keys(0, 1, 2, 2)
        quantise_projected()
        project_keys(1, 0, 0, 2)
        quantise_projected()
        turn("R1", 0, nc.scalar.copy)
        turn("R1", 1, nc.vector.tensor_copy)
        turn("R1", 2, nc.scalar.copy)
        turn("R1", 3, nc.scalar.copy)
        split_row("Q0", 0)
        split_row("Q0", 1)
        split_row("Q0", 2)
        split_row("Q0", 3)
        quantise("R1", 0, 4)
        project_keys(1, 0, 2, 2)
        quantise_projected()
        project_keys(1, 1, 0, 2)
        quantise_projected()
        turn("Q0", 0, nc.scalar.copy)
        turn("Q0", 1, nc.vector.tensor_copy)
        turn("Q0", 2, nc.scalar.copy)
        turn("Q0", 3, nc.scalar.copy)
        split_row("Q1", 0)
        split_row("Q1", 1)
        split_row("Q1", 2)
        split_row("Q1", 3)
        quantise("Q0", 0, 4)
        project_keys(1, 1, 2, 2)
        quantise_projected()
        turn("Q1", 0, nc.scalar.copy)
        turn("Q1", 1, nc.vector.tensor_copy)
        turn("Q1", 2, nc.scalar.copy)
        turn("Q1", 3, nc.scalar.copy)
        quantise("Q1", 0, 4)
        project_query(0, 0)
        quantise_projected()
        project_query(0, 1)
        quantise_projected()
        project_query(1, 0)
        quantise_projected()
        project_query(1, 1)
        quantise_projected()
        bank0 = scores(0)
        mask_scores(0, bank0)
        row_maximum(0)
        project_query(2, 0)
        quantise_projected()
        project_query(2, 1)
        bank1 = scores(1)
        exponentials(0)
        mask_scores(1, bank1)
        quantise_projected()
        row_maximum(1)
        invert_row_sum(0)
        normalise_and_store(0, True)
        project_query(3, 0)
        quantise_projected()
        project_query(3, 1)
        bank2 = scores(2)
        exponentials(1)
        mask_scores(2, bank2)
        quantise_projected()
        row_maximum(2)
        invert_row_sum(1)
        normalise_and_store(1, True)
        project_query(4, 0)
        quantise_projected()
        project_query(4, 1)
        bank3 = scores(3)
        exponentials(2)
        mask_scores(3, bank3)
        quantise_projected()
        row_maximum(3)
        invert_row_sum(2)
        normalise_and_store(2, True)
        project_query(5, 0)
        quantise_projected()
        project_query(5, 1)
        bank4 = scores(4)
        exponentials(3)
        mask_scores(4, bank4)
        quantise_projected()
        row_maximum(4)
        invert_row_sum(3)
        normalise_and_store(3, True)
        project_query(6, 0)
        quantise_projected()
        project_query(6, 1)
        bank5 = scores(5)
        exponentials(4)
        mask_scores(5, bank5)
        quantise_projected()
        row_maximum(5)
        invert_row_sum(4)
        normalise_and_store(4, True)
        project_query(7, 0)
        quantise_projected()
        project_query(7, 1)
        bank6 = scores(6)
        exponentials(5)
        mask_scores(6, bank6)
        quantise_projected()
        row_maximum(6)
        invert_row_sum(5)
        normalise_and_store(5, True)
        bank7 = scores(7)
        exponentials(6)
        mask_scores(7, bank7)
        row_maximum(7)
        invert_row_sum(6)
        normalise_and_store(6, False)
        exponentials(7)
        invert_row_sum(7)
        normalise_and_store(7, False)
